import numpy as np
import ml_dtypes


def mxq(x, axis, fmt="e4m3"):
    dtype, down = {"e4m3": (ml_dtypes.float8_e4m3fn, 7), "e5m2": (ml_dtypes.float8_e5m2, 14)}[fmt]
    v = np.moveaxis(np.asarray(x, np.float32).astype(ml_dtypes.bfloat16).astype(np.float64), axis, -1)
    blocks = v.reshape(v.shape[:-1] + (-1, 32))
    amax = np.abs(blocks).max(-1, keepdims=True)
    byte = np.maximum(np.where(amax > 0, np.frexp(amax)[1] - 1 + 127, 0) - down, 1)
    scale = np.exp2(byte - 127.0)
    codes = (blocks / scale).astype(np.float32).astype(dtype).astype(np.float64)
    return np.moveaxis((codes * scale).reshape(v.shape), -1, axis)


WIDE = False


def mx_kscale(k):
    if not WIDE:
        return np.ones(k)
    levels = np.array([10, -10, 5, -5, 0])
    if k % 512:
        return np.exp2(np.random.permutation(np.resize(levels, k // 32))).repeat(32)
    a = np.empty((k // 512, 16))
    for p in range(k // 512):
        a[p, :8] = np.random.permutation(np.resize(levels, 8))
        for g in range(8):
            far = levels[np.abs(levels - a[p, g]) >= 10]
            a[p, g + 8] = far[np.random.randint(len(far))]
    return np.exp2(a.ravel()).repeat(32)


BF16 = ml_dtypes.bfloat16


def bf(x):
    return np.asarray(x, np.float32).astype(BF16)


def f64(x):
    return np.asarray(x).astype(np.float64)


B, L, D, F, K = 1024, 8, 512, 512, 16
EPS = 1e-12


def silu(v):
    return v / (1.0 + np.exp(-v))


def l2norm(t, axis):
    n = np.sqrt((t * t).sum(axis=axis, keepdims=True))
    return t / np.maximum(n, EPS)


def mix_draw(rows, cols):
    return np.random.standard_normal((L, rows, cols)) * np.sqrt(np.e / K) * np.exp(0.5 * np.random.standard_normal((L, 1, cols)))


def hidden_draw():
    return silu(3.0 * np.random.standard_normal((B, L, F))) * np.random.standard_normal((B, L, F)) * 3.0 / np.sqrt(D)


def setup_inputs():
    t = mx_kscale(F)
    g = np.sqrt(np.mean(1.0 / t**2))
    return {"h": bf(hidden_draw() * t * g),
            "w_down_mix": bf(mix_draw(F, D) / t[:, None])}


def reference(h, w_down_mix):
    wd = l2norm(f64(w_down_mix), 1)
    y = mxq(f64(h).transpose(1, 0, 2), 2, "e4m3") @ mxq(wd, 1, "e4m3")
    return l2norm(y, -1).transpose(1, 0, 2)

@@ -1,0 +1,250 @@
+from contextlib import ExitStack
+
+import concourse.mybir as mybir
+from concourse.masks import make_identity
+
+F32 = mybir.dt.float32
+BF16 = mybir.dt.bfloat16
+U32 = mybir.dt.uint32
+U8 = mybir.dt.uint8
+FP8X4 = mybir.dt.float8_e4m3fn_x4
+ACT = mybir.ActivationFunctionType
+ALU = mybir.AluOpType
+
+P = 128
+BATCH = 1024
+TOKENS = 8
+HIDDEN = 512
+FEATURES = 512
+PACK = 4
+EPS = 1e-12
+
+BATCH_TILES = BATCH // P
+COLUMN_BLOCKS = FEATURES // P
+TOKEN_PAIRS = TOKENS // 2
+WORDS = HIDDEN // 2
+GROUP = 4
+GROUPS_PER_TILE = TOKENS // GROUP
+GROUPS = BATCH_TILES * GROUPS_PER_TILE
+STORE_TOKENS = 2
+TILES_REGROUPED_BY_VECTOR = 2
+
+FLOPS = 2 * BATCH * TOKENS * HIDDEN * FEATURES
+
+
+def tile_npertokenswishglu_basis_pb_t_kernel(tc, h, w_down_mix, out):
+    nc = tc.nc
+    with ExitStack() as ctx:
+        ctx.enter_context(tc.manual_schedule())
+        const = ctx.enter_context(tc.tile_pool(name="const", bufs=1))
+        raw = ctx.enter_context(tc.tile_pool(name="raw", bufs=1))
+        operands = ctx.enter_context(tc.tile_pool(name="operands", bufs=1))
+        stage = ctx.enter_context(tc.tile_pool(name="stage", bufs=2))
+        small = ctx.enter_context(tc.tile_pool(name="small", bufs=3))
+        results = ctx.enter_context(tc.tile_pool(name="results", bufs=4))
+
+        w_raw = []
+        h_raw = []
+        for n in range(TOKENS):
+            w_tile = raw.tile([P, PACK, FEATURES], BF16, name="w_raw%d" % n)
+            nc.sync.dma_start(out=w_tile[:], in_=w_down_mix[n].rearrange("(q t) j -> q t j", t=PACK))
+            w_raw.append(w_tile)
+            h_tile = raw.tile([P, TOKENS * HIDDEN], BF16, name="h_raw%d" % n)
+            nc.sync.dma_start(out=h_tile[:], in_=h[n * P : (n + 1) * P].rearrange("b l f -> b (l f)"))
+            h_raw.append(h_tile)
+
+        ident_bf16 = const.tile([P, P], BF16)
+        make_identity(nc, ident_bf16[:])
+        ident_f32 = const.tile([P, P], F32)
+        make_identity(nc, ident_f32[:])
+
+        one = const.tile([P, 1], F32)
+        nc.vector.memset(one[:], 1.0)
+        warm = const.tile([P, 1], F32)
+        nc.scalar.activation(out=warm[:], in_=one[:], func=ACT.Abs_reciprocal_sqrt)
+
+        w_codes = [operands.tile([P, FEATURES], U32, name="w_codes%d" % l, align_bytes=64) for l in range(TOKENS)]
+        w_scales = [operands.tile([P, FEATURES], U8, name="w_scales%d" % l, align_bytes=64) for l in range(TOKENS)]
+        h_codes = [operands.tile([P, TOKENS * P], U32, name="h_codes%d" % i, align_bytes=64) for i in range(BATCH_TILES)]
+        h_scales = [operands.tile([P, TOKENS * P], U8, name="h_scales%d" % i, align_bytes=64) for i in range(BATCH_TILES)]
+
+        def sum_of_squares(values, total):
+            squares = stage.tile([P, HIDDEN], BF16, name="squares", bufs=4)
+            nc.scalar.activation(out=squares[:], in_=values, func=ACT.Square, accum_out=total)
+
+        def clamp(totals, width):
+            clamped = small.tile([P, width], F32, name="clamped")
+            nc.vector.tensor_scalar_max(out=clamped[:], in0=totals[:], scalar1=EPS * EPS)
+            return clamped
+
+        def inverse_root(clamped, width):
+            inverse_norm = small.tile([P, width], F32, name="inverse_norm")
+            nc.scalar.activation(out=inverse_norm[:], in_=clamped[:], func=ACT.Abs_reciprocal_sqrt)
+            return inverse_norm
+
+        with tc.psum_pool(name="prep_psum", bufs=2) as prep_psum:
+            w_flipped = {}
+            w_totals = {}
+            w_inverse_norm = {}
+            w_spread = {}
+            nd = {}
+            h_flipped = {}
+            h_grouped = {}
+
+            def flip_weight(l):
+                for half in range(2):
+                    w_flipped[l, half] = prep_psum.tile([P, 2, PACK, P], BF16, name="w_flipped", bufs=2)
+                    for k in range(2):
+                        block = 2 * half + k
+                        for t in range(PACK):
+                            nc.tensor.transpose(
+                                out=w_flipped[l, half][:, k, t, :],
+                                in_=w_raw[l][:, t, block * P : (block + 1) * P],
+                                identity=ident_bf16[:],
+                            )
+
+            def weight_column_sums(l):
+                w_totals[l] = small.tile([P, COLUMN_BLOCKS], F32, name="w_totals")
+                for block in range(COLUMN_BLOCKS):
+                    sum_of_squares(
+                        w_flipped[l, block // 2][:, block % 2].rearrange("j t q -> j (t q)"),
+                        w_totals[l][:, block : block + 1],
+                    )
+
+            def spread_weight_norms(l):
+                w_spread[l] = prep_psum.tile([P, FEATURES], F32, name="w_spread", bufs=2)
+                for block in range(COLUMN_BLOCKS):
+                    nc.tensor.matmul(
+                        out=w_spread[l][:, block * P : (block + 1) * P],
+                        lhsT=w_inverse_norm[l][:, block : block + 1].to_broadcast([P, P]),
+                        rhs=ident_f32[:],
+                        start=True,
+                        stop=True,
+                    )
+
+            def normalise_weight(l):
+                nd[l] = stage.tile([P, FEATURES, PACK], BF16, name="nd", align_bytes=64)
+                nc.vector.tensor_tensor(
+                    out=nd[l][:],
+                    in0=w_raw[l][:].rearrange("q t j -> q j t"),
+                    in1=w_spread[l][:].unsqueeze(2).to_broadcast([P, FEATURES, PACK]),
+                    op=ALU.mult,
+                )
+
+            def quantise_weight(l):
+                nc.vector.quantize_mx(
+                    out=w_codes[l][:].bitcast(FP8X4),
+                    scales=w_scales[l][:],
+                    in_=nd[l][:].rearrange("q j t -> q (j t)"),
+                )
+
+            def flip_h(i):
+                h_words = h_raw[i][:].bitcast(F32)
+                for pair in range(TOKEN_PAIRS):
+                    h_flipped[i, pair] = prep_psum.tile([P, 2, 2, P], F32, name="h_flipped", bufs=4)
+                    for k in range(2):
+                        for u in range(2):
+                            token = 2 * pair + k
+                            nc.tensor.transpose(
+                                out=h_flipped[i, pair][:, k, u, :],
+                                in_=h_words[:, token * WORDS + u : (token + 1) * WORDS : 2],
+                                identity=ident_f32[:],
+                            )
+
+            def regroup_h(i):
+                h_grouped[i] = stage.tile([P, TOKENS * P * PACK], BF16, name="h_grouped", align_bytes=64, bufs=3)
+                grouped_words = h_grouped[i][:].bitcast(F32)
+                copy = nc.vector.tensor_copy if i < TILES_REGROUPED_BY_VECTOR else nc.scalar.copy
+                bank_words = 2 * P * 2
+                for pair in range(TOKEN_PAIRS):
+                    copy(
+                        out=grouped_words[:, pair * bank_words : (pair + 1) * bank_words].rearrange(
+                            "q (k b u) -> q k b u", k=2, u=2
+                        ),
+                        in_=h_flipped[i, pair][:].rearrange("q k u b -> q k b u"),
+                    )
+
+            def quantise_h(i, half):
+                width = GROUP * P
+                nc.vector.quantize_mx(
+                    out=h_codes[i][:, half * width : (half + 1) * width].bitcast(FP8X4),
+                    scales=h_scales[i][:, half * width : (half + 1) * width],
+                    in_=h_grouped[i][:, half * width * PACK : (half + 1) * width * PACK],
+                )
+
+            for n in range(TOKENS + 2):
+                newest = n
+                middle = n - 1
+                oldest = n - 2
+                if newest < TOKENS:
+                    flip_weight(newest)
+                if oldest >= 0:
+                    spread_weight_norms(oldest)
+                if newest < TOKENS:
+                    flip_h(newest)
+                    weight_column_sums(newest)
+                if 0 <= middle < TOKENS:
+                    w_inverse_norm[middle] = inverse_root(clamp(w_totals[middle], COLUMN_BLOCKS), COLUMN_BLOCKS)
+                    quantise_h(middle, 0)
+                if oldest >= 0:
+                    normalise_weight(oldest)
+                if 0 <= middle < TOKENS:
+                    quantise_h(middle, 1)
+                if newest < TOKENS:
+                    regroup_h(newest)
+                if oldest >= 0:
+                    quantise_weight(oldest)
+
+        with tc.psum_pool(name="y_psum", bufs=2 * GROUP, reuse_waits="tile") as y_psum:
+            y = {}
+            y_totals = {}
+            y_clamped = {}
+            y_inverse_norm = {}
+            normed = {}
+
+            def multiply(g):
+                i = g // GROUPS_PER_TILE
+                for k in range(GROUP):
+                    l = (g % GROUPS_PER_TILE) * GROUP + k
+                    y[g, k] = y_psum.tile([P, FEATURES], F32, name="y")
+                    nc.tensor.matmul_mx(
+                        out=y[g, k][:],
+                        lhsT=h_codes[i][:, l * P : (l + 1) * P].bitcast(FP8X4),
+                        lhsT_scale=h_scales[i][:, l * P : (l + 1) * P],
+                        rhs=w_codes[l][:].bitcast(FP8X4),
+                        rhs_scale=w_scales[l][:],
+                        start=True,
+                        stop=True,
+                    )
+
+            def row_sum(g, k):
+                sum_of_squares(y[g, k][:], y_totals[g][:, k : k + 1])
+
+            def scale_rows(g, k):
+                nc.vector.tensor_scalar_mul(
+                    out=normed[g][:, k, :], in0=y[g, k][:], scalar1=y_inverse_norm[g][:, k : k + 1]
+                )
+                if k % STORE_TOKENS == STORE_TOKENS - 1:
+                    i = g // GROUPS_PER_TILE
+                    last_token = (g % GROUPS_PER_TILE) * GROUP + k
+                    nc.sync.dma_start(
+                        out=out[i * P : (i + 1) * P, last_token + 1 - STORE_TOKENS : last_token + 1, :],
+                        in_=normed[g][:, k + 1 - STORE_TOKENS : k + 1, :],
+                    )
+
+            for g in range(GROUPS + 1):
+                if g < GROUPS:
+                    multiply(g)
+                    y_totals[g] = small.tile([P, GROUP], F32, name="y_totals")
+                    row_sum(g, 0)
+                if g >= 1:
+                    y_inverse_norm[g - 1] = inverse_root(y_clamped[g - 1], GROUP)
+                    normed[g - 1] = results.tile([P, GROUP, FEATURES], F32, name="normed")
+                    for k in range(GROUP - 1):
+                        scale_rows(g - 1, k)
+                if g < GROUPS:
+                    for k in range(1, GROUP):
+                        row_sum(g, k)
+                    y_clamped[g] = clamp(y_totals[g], GROUP)
+                if g >= 1:
+                    scale_rows(g - 1, GROUP - 1)

@@ -19,17 +19,24 @@ FEATURES = 512
 PACK = 4
 EPS = 1e-12
 
-BATCH_TILES = BATCH // P
-COLUMN_BLOCKS = FEATURES // P
-TOKEN_PAIRS = TOKENS // 2
+TILES = BATCH // P
+BLOCKS = FEATURES // P
+PAIR = 2
+PAIRS = TOKENS // PAIR
+UNITS = PAIRS * TILES
 WORDS = HIDDEN // 2
-GROUP = 4
-GROUPS_PER_TILE = TOKENS // GROUP
-GROUPS = BATCH_TILES * GROUPS_PER_TILE
-STORE_TOKENS = 2
-TILES_REGROUPED_BY_VECTOR = 2
 
 FLOPS = 2 * BATCH * TOKENS * HIDDEN * FEATURES
+
+GROUP = 4
+GROUPS_PER_TILE = TOKENS // GROUP
+GROUPS = TILES * GROUPS_PER_TILE
+STORE_TOKENS = 2
+
+WEIGHTS_FIRST = 6
+DIAGONAL_AT = dict(gram=(0, 1, 2, 3), mask=4, ones=(6, 6, 7, 7), root=8, scale=(8, 9, 10, 11), quantise=13)
+TURNED_AT = dict(flip=(1, 1, 5, 5), square=(2, 3, 6, 7), root=9, spread=(11, 11, 12, 12), scale=(12, 13, 14, 15), quantise=17)
+H_REGROUP, H_QUANTISE = 1, 2
 
 
 def tile_npertokenswishglu_basis_pb_t_kernel(tc, h, w_down_mix, out):
@@ -38,96 +45,149 @@ def tile_npertokenswishglu_basis_pb_t_kernel(tc, h, w_down_mix, out):
         ctx.enter_context(tc.manual_schedule())
         const = ctx.enter_context(tc.tile_pool(name="const", bufs=1))
         raw = ctx.enter_context(tc.tile_pool(name="raw", bufs=1))
-        operands = ctx.enter_context(tc.tile_pool(name="operands", bufs=1))
+        weights = ctx.enter_context(tc.tile_pool(name="weights", bufs=1))
         stage = ctx.enter_context(tc.tile_pool(name="stage", bufs=2))
-        small = ctx.enter_context(tc.tile_pool(name="small", bufs=3))
-        results = ctx.enter_context(tc.tile_pool(name="results", bufs=4))
+        small = ctx.enter_context(tc.tile_pool(name="small", bufs=4))
+        results = ctx.enter_context(tc.tile_pool(name="results", bufs=6))
 
-        w_raw = []
-        h_raw = []
-        for n in range(TOKENS):
-            w_tile = raw.tile([P, PACK, FEATURES], BF16, name="w_raw%d" % n)
-            nc.sync.dma_start(out=w_tile[:], in_=w_down_mix[n].rearrange("(q t) j -> q t j", t=PACK))
-            w_raw.append(w_tile)
-            h_tile = raw.tile([P, TOKENS * HIDDEN], BF16, name="h_raw%d" % n)
-            nc.sync.dma_start(out=h_tile[:], in_=h[n * P : (n + 1) * P].rearrange("b l f -> b (l f)"))
-            h_raw.append(h_tile)
+        w_raw = {}
+        h_raw = {}
+
+        def load_weight(l):
+            w_raw[l] = raw.tile([P, PACK, FEATURES], BF16, name="w_raw%d" % l)
+            nc.sync.dma_start(out=w_raw[l][:], in_=w_down_mix[l].rearrange("(q t) j -> q t j", t=PACK))
+
+        def load_h(i, pair, count):
+            width = PAIR * HIDDEN
+            tile = raw.tile([P, count * width], BF16, name="h_raw%d_%d" % (i, pair))
+            nc.sync.dma_start(
+                out=tile[:].rearrange("b (l f) -> b l f", f=HIDDEN),
+                in_=h[i * P : (i + 1) * P, PAIR * pair : PAIR * (pair + count), :],
+            )
+            for k in range(count):
+                h_raw[i * PAIRS + pair + k] = tile[:, k * width : (k + 1) * width]
+
+        load_weight(0)
+        load_weight(1)
+        load_h(0, 0, 2)
+        load_h(0, 2, 2)
+        for i in range(1, TILES):
+            if PAIR * i < TOKENS:
+                load_weight(PAIR * i)
+                load_weight(PAIR * i + 1)
+            load_h(i, 0, PAIRS)
 
         ident_bf16 = const.tile([P, P], BF16)
         make_identity(nc, ident_bf16[:])
         ident_f32 = const.tile([P, P], F32)
         make_identity(nc, ident_f32[:])
+        ones = const.tile([P, P], F32)
+        nc.vector.memset(ones[:], 1.0)
 
-        one = const.tile([P, 1], F32)
-        nc.vector.memset(one[:], 1.0)
         warm = const.tile([P, 1], F32)
-        nc.scalar.activation(out=warm[:], in_=one[:], func=ACT.Abs_reciprocal_sqrt)
-
-        w_codes = [operands.tile([P, FEATURES], U32, name="w_codes%d" % l, align_bytes=64) for l in range(TOKENS)]
-        w_scales = [operands.tile([P, FEATURES], U8, name="w_scales%d" % l, align_bytes=64) for l in range(TOKENS)]
-        h_codes = [operands.tile([P, TOKENS * P], U32, name="h_codes%d" % i, align_bytes=64) for i in range(BATCH_TILES)]
-        h_scales = [operands.tile([P, TOKENS * P], U8, name="h_scales%d" % i, align_bytes=64) for i in range(BATCH_TILES)]
+        nc.scalar.activation(out=warm[:], in_=ones[:, 0:1], func=ACT.Abs_reciprocal_sqrt)
 
         def sum_of_squares(values, total):
             squares = stage.tile([P, HIDDEN], BF16, name="squares", bufs=4)
             nc.scalar.activation(out=squares[:], in_=values, func=ACT.Square, accum_out=total)
 
         def clamp(totals, width):
-            clamped = small.tile([P, width], F32, name="clamped")
+            clamped = small.tile([P, width], F32, name="clamped%d" % width)
             nc.vector.tensor_scalar_max(out=clamped[:], in0=totals[:], scalar1=EPS * EPS)
             return clamped
 
         def inverse_root(clamped, width):
-            inverse_norm = small.tile([P, width], F32, name="inverse_norm")
-            nc.scalar.activation(out=inverse_norm[:], in_=clamped[:], func=ACT.Abs_reciprocal_sqrt)
-            return inverse_norm
+            inverse = small.tile([P, width], F32, name="inverse%d" % width)
+            nc.scalar.activation(out=inverse[:], in_=clamped[:], func=ACT.Abs_reciprocal_sqrt)
+            return inverse
 
-        with tc.psum_pool(name="prep_psum", bufs=2) as prep_psum:
-            w_flipped = {}
+        w_codes = [weights.tile([P, FEATURES], U32, name="w_codes%d" % l, align_bytes=64) for l in range(TOKENS)]
+        w_scales = [weights.tile([P, FEATURES], U8, name="w_scales%d" % l, align_bytes=64) for l in range(TOKENS)]
+        h_codes = [weights.tile([P, TOKENS * P], U32, name="h_codes%d" % i, align_bytes=64) for i in range(TILES)]
+        h_scales = [weights.tile([P, TOKENS * P], U8, name="h_scales%d" % i, align_bytes=64) for i in range(TILES)]
+
+        with tc.psum_pool(name="prep_psum", bufs=1) as psum:
+            w_psum = {}
             w_totals = {}
-            w_inverse_norm = {}
-            w_spread = {}
+            w_diagonal = {}
+            w_inverse = {}
             nd = {}
-            h_flipped = {}
-            h_grouped = {}
 
-            def flip_weight(l):
-                for half in range(2):
-                    w_flipped[l, half] = prep_psum.tile([P, 2, PACK, P], BF16, name="w_flipped", bufs=2)
-                    for k in range(2):
-                        block = 2 * half + k
-                        for t in range(PACK):
-                            nc.tensor.transpose(
-                                out=w_flipped[l, half][:, k, t, :],
-                                in_=w_raw[l][:, t, block * P : (block + 1) * P],
-                                identity=ident_bf16[:],
-                            )
-
-            def weight_column_sums(l):
-                w_totals[l] = small.tile([P, COLUMN_BLOCKS], F32, name="w_totals")
-                for block in range(COLUMN_BLOCKS):
-                    sum_of_squares(
-                        w_flipped[l, block // 2][:, block % 2].rearrange("j t q -> j (t q)"),
-                        w_totals[l][:, block : block + 1],
+            def flip_weight(l, block):
+                if block % 2 == 0:
+                    w_psum[l, block // 2] = psum.tile([P, 2, PACK, P], BF16, name="w_flipped", bufs=1)
+                for t in range(PACK):
+                    nc.tensor.transpose(
+                        out=w_psum[l, block // 2][:, block % 2, t, :],
+                        in_=w_raw[l][:, t, block * P : (block + 1) * P],
+                        identity=ident_bf16[:],
                     )
 
-            def spread_weight_norms(l):
-                w_spread[l] = prep_psum.tile([P, FEATURES], F32, name="w_spread", bufs=2)
-                for block in range(COLUMN_BLOCKS):
+            def square_weight(l, block):
+                if block == 0:
+                    w_totals[l] = small.tile([P, BLOCKS], F32, name="w_totals")
+                sum_of_squares(
+                    w_psum[l, block // 2][:, block % 2].rearrange("j t q -> j (t q)"), w_totals[l][:, block : block + 1]
+                )
+
+            def root_turned(l):
+                w_inverse[l] = inverse_root(clamp(w_totals[l], BLOCKS), BLOCKS)
+
+            def spread_turned(l, block):
+                if block == 0:
+                    w_psum[l] = psum.tile([P, FEATURES], F32, name="w_spread", bufs=1)
+                nc.tensor.matmul(
+                    out=w_psum[l][:, block * P : (block + 1) * P],
+                    lhsT=w_inverse[l][:, block : block + 1].to_broadcast([P, P]),
+                    rhs=ident_f32[:],
+                    start=True,
+                    stop=True,
+                )
+
+            def gram(l, block):
+                if block == 0:
+                    w_psum[l] = psum.tile([P, BLOCKS, P], F32, name="w_sums", bufs=2)
+                for t in range(PACK):
+                    columns = w_raw[l][:, t, block * P : (block + 1) * P]
                     nc.tensor.matmul(
-                        out=w_spread[l][:, block * P : (block + 1) * P],
-                        lhsT=w_inverse_norm[l][:, block : block + 1].to_broadcast([P, P]),
-                        rhs=ident_f32[:],
-                        start=True,
-                        stop=True,
+                        out=w_psum[l][:, block, :], lhsT=columns, rhs=columns, start=t == 0, stop=t == PACK - 1
                     )
 
-            def normalise_weight(l):
-                nd[l] = stage.tile([P, FEATURES, PACK], BF16, name="nd", align_bytes=64)
+            def mask(l):
+                w_diagonal[l] = stage.tile([P, BLOCKS, P], F32, name="w_diagonal")
+                nc.vector.scalar_tensor_tensor(
+                    out=w_diagonal[l][:],
+                    in0=w_psum[l][:],
+                    scalar=EPS * EPS,
+                    in1=ident_f32[:].unsqueeze(1).to_broadcast([P, BLOCKS, P]),
+                    op0=ALU.max,
+                    op1=ALU.mult,
+                )
+
+            def add_partitions(l, block):
+                if block == 0:
+                    w_psum[l] = psum.tile([P, FEATURES], F32, name="w_sums", bufs=2)
+                nc.tensor.matmul(
+                    out=w_psum[l][:, block * P : (block + 1) * P],
+                    lhsT=ones[:],
+                    rhs=w_diagonal[l][:, block, :],
+                    start=True,
+                    stop=True,
+                )
+
+            def root_gram(l):
+                w_inverse[l] = stage.tile([P, FEATURES], F32, name="w_inverse")
+                nc.scalar.activation(out=w_inverse[l][:], in_=w_psum[l][:], func=ACT.Abs_reciprocal_sqrt)
+
+            def scale_weight(l, block):
+                if block == 0:
+                    nd[l] = stage.tile([P, FEATURES, PACK], BF16, name="nd", align_bytes=64)
+                columns = slice(block * P, (block + 1) * P)
+                inverse = w_inverse[l] if l % 2 == 0 else w_psum[l]
                 nc.vector.tensor_tensor(
-                    out=nd[l][:],
-                    in0=w_raw[l][:].rearrange("q t j -> q j t"),
-                    in1=w_spread[l][:].unsqueeze(2).to_broadcast([P, FEATURES, PACK]),
+                    out=nd[l][:, columns, :],
+                    in0=w_raw[l][:].rearrange("q t j -> q j t")[:, columns, :],
+                    in1=inverse[:, columns].unsqueeze(2).to_broadcast([P, P, PACK]),
                     op=ALU.mult,
                 )
 
@@ -138,62 +198,75 @@ def tile_npertokenswishglu_basis_pb_t_kernel(tc, h, w_down_mix, out):
                     in_=nd[l][:].rearrange("q j t -> q (j t)"),
                 )
 
-            def flip_h(i):
-                h_words = h_raw[i][:].bitcast(F32)
-                for pair in range(TOKEN_PAIRS):
-                    h_flipped[i, pair] = prep_psum.tile([P, 2, 2, P], F32, name="h_flipped", bufs=4)
-                    for k in range(2):
-                        for u in range(2):
-                            token = 2 * pair + k
-                            nc.tensor.transpose(
-                                out=h_flipped[i, pair][:, k, u, :],
-                                in_=h_words[:, token * WORDS + u : (token + 1) * WORDS : 2],
-                                identity=ident_f32[:],
-                            )
+            def weight_work(engine, step):
+                for l in range(TOKENS):
+                    at = DIAGONAL_AT if l % 2 == 0 else TURNED_AT
+                    s = step + WEIGHTS_FIRST - (l // PAIR) * 2 * PAIRS
+                    blocks = range(BLOCKS)
+                    if engine == "tensor":
+                        for name, work in (("gram", gram), ("ones", add_partitions), ("spread", spread_turned), ("flip", flip_weight)):
+                            for block in blocks:
+                                if name in at and at[name][block] == s:
+                                    work(l, block)
+                    elif engine == "scalar":
+                        for block in blocks:
+                            if "square" in at and at["square"][block] == s:
+                                square_weight(l, block)
+                        if at["root"] == s:
+                            if l % 2 == 0:
+                                root_gram(l)
+                            else:
+                                root_turned(l)
+                    else:
+                        if at.get("mask") == s:
+                            mask(l)
+                        for block in blocks:
+                            if at["scale"][block] == s:
+                                scale_weight(l, block)
+                        if at["quantise"] == s:
+                            quantise_weight(l)
 
-            def regroup_h(i):
-                h_grouped[i] = stage.tile([P, TOKENS * P * PACK], BF16, name="h_grouped", align_bytes=64, bufs=3)
-                grouped_words = h_grouped[i][:].bitcast(F32)
-                copy = nc.vector.tensor_copy if i < TILES_REGROUPED_BY_VECTOR else nc.scalar.copy
-                bank_words = 2 * P * 2
-                for pair in range(TOKEN_PAIRS):
-                    copy(
-                        out=grouped_words[:, pair * bank_words : (pair + 1) * bank_words].rearrange(
-                            "q (k b u) -> q k b u", k=2, u=2
-                        ),
-                        in_=h_flipped[i, pair][:].rearrange("q k u b -> q k b u"),
-                    )
+            h_flipped = {}
+            h_grouped = {}
 
-            def quantise_h(i, half):
-                width = GROUP * P
-                nc.vector.quantize_mx(
-                    out=h_codes[i][:, half * width : (half + 1) * width].bitcast(FP8X4),
-                    scales=h_scales[i][:, half * width : (half + 1) * width],
-                    in_=h_grouped[i][:, half * width * PACK : (half + 1) * width * PACK],
+            def flip_h(u):
+                h_flipped[u] = psum.tile([P, PAIR, 2, P], F32, name="h_flipped", bufs=4)
+                words = h_raw[u].bitcast(F32)
+                for k in range(PAIR):
+                    for e in range(2):
+                        nc.tensor.transpose(
+                            out=h_flipped[u][:, k, e, :],
+                            in_=words[:, k * WORDS + e : (k + 1) * WORDS : 2],
+                            identity=ident_f32[:],
+                        )
+
+            def regroup_h(u):
+                h_grouped[u] = stage.tile([P, PAIR * P * PACK], BF16, name="h_grouped", align_bytes=64, bufs=4)
+                nc.scalar.copy(
+                    out=h_grouped[u][:].bitcast(F32).rearrange("q (k b e) -> q k b e", k=PAIR, e=2),
+                    in_=h_flipped[u][:].rearrange("q k e b -> q k b e"),
                 )
 
-            for n in range(TOKENS + 2):
-                newest = n
-                middle = n - 1
-                oldest = n - 2
-                if newest < TOKENS:
-                    flip_weight(newest)
-                if oldest >= 0:
-                    spread_weight_norms(oldest)
-                if newest < TOKENS:
-                    flip_h(newest)
-                    weight_column_sums(newest)
-                if 0 <= middle < TOKENS:
-                    w_inverse_norm[middle] = inverse_root(clamp(w_totals[middle], COLUMN_BLOCKS), COLUMN_BLOCKS)
-                    quantise_h(middle, 0)
-                if oldest >= 0:
-                    normalise_weight(oldest)
-                if 0 <= middle < TOKENS:
-                    quantise_h(middle, 1)
-                if newest < TOKENS:
-                    regroup_h(newest)
-                if oldest >= 0:
-                    quantise_weight(oldest)
+            def quantise_h(u):
+                columns = slice((u % PAIRS) * PAIR * P, (u % PAIRS + 1) * PAIR * P)
+                nc.vector.quantize_mx(
+                    out=h_codes[u // PAIRS][:, columns].bitcast(FP8X4),
+                    scales=h_scales[u // PAIRS][:, columns],
+                    in_=h_grouped[u][:],
+                )
+
+
+            last = (PAIRS - 1) * 2 * PAIRS - WEIGHTS_FIRST + TURNED_AT["quantise"]
+            for step in range(-WEIGHTS_FIRST, max(UNITS + H_QUANTISE, last + 1)):
+                if 0 <= step < UNITS:
+                    flip_h(step)
+                weight_work("tensor", step)
+                if 0 <= step - H_REGROUP < UNITS:
+                    regroup_h(step - H_REGROUP)
+                weight_work("scalar", step)
+                if 0 <= step - H_QUANTISE < UNITS:
+                    quantise_h(step - H_QUANTISE)
+                weight_work("vector", step)
 
         with tc.psum_pool(name="y_psum", bufs=2 * GROUP, reuse_waits="tile") as y_psum:
             y = {}

@@ -36,6 +36,7 @@ STORE_TOKENS = 2
 WEIGHTS_FIRST = 6
 DIAGONAL_AT = dict(gram=(0, 1, 2, 3), mask=4, ones=(6, 6, 7, 7), root=8, scale=(8, 9, 10, 11), quantise=13)
 TURNED_AT = dict(flip=(1, 1, 5, 5), square=(2, 3, 6, 7), root=9, spread=(11, 11, 12, 12), scale=(12, 13, 14, 15), quantise=17)
+RUN = 4
 H_REGROUP, H_QUANTISE = 1, 2
 
 
@@ -185,9 +186,12 @@ def tile_npertokenswishglu_basis_pb_t_kernel(tc, h, w_down_mix, out):
                 columns = slice(block * P, (block + 1) * P)
                 inverse = w_inverse[l] if l % 2 == 0 else w_psum[l]
                 nc.vector.tensor_tensor(
-                    out=nd[l][:, columns, :],
-                    in0=w_raw[l][:].rearrange("q t j -> q j t")[:, columns, :],
-                    in1=inverse[:, columns].unsqueeze(2).to_broadcast([P, P, PACK]),
+                    out=nd[l][:, columns, :].rearrange("q (c i) t -> q c t i", i=RUN),
+                    in0=w_raw[l][:, :, columns].rearrange("q t (c i) -> q c t i", i=RUN),
+                    in1=inverse[:, columns]
+                    .rearrange("q (c i) -> q c i", i=RUN)
+                    .unsqueeze(2)
+                    .to_broadcast([P, P // RUN, PACK, RUN]),
                     op=ALU.mult,
                 )
 

@@ -37,6 +37,7 @@ WEIGHTS_FIRST = 6
 DIAGONAL_AT = dict(gram=(0, 1, 2, 3), mask=4, ones=(6, 6, 7, 7), root=8, scale=(8, 9, 10, 11), quantise=13)
 TURNED_AT = dict(flip=(1, 1, 5, 5), square=(2, 3, 6, 7), root=9, spread=(11, 11, 12, 12), scale=(12, 13, 14, 15), quantise=17)
 RUN = 4
+H_SHARE = 11 / 16
 H_REGROUP, H_QUANTISE = 1, 2
 
 
@@ -49,7 +50,7 @@ def tile_npertokenswishglu_basis_pb_t_kernel(tc, h, w_down_mix, out):
         weights = ctx.enter_context(tc.tile_pool(name="weights", bufs=1))
         stage = ctx.enter_context(tc.tile_pool(name="stage", bufs=2))
         small = ctx.enter_context(tc.tile_pool(name="small", bufs=4))
-        results = ctx.enter_context(tc.tile_pool(name="results", bufs=6))
+        results = ctx.enter_context(tc.tile_pool(name="results", bufs=4))
 
         w_raw = {}
         h_raw = {}
@@ -245,7 +246,7 @@ def tile_npertokenswishglu_basis_pb_t_kernel(tc, h, w_down_mix, out):
                         )
 
             def regroup_h(u):
-                h_grouped[u] = stage.tile([P, PAIR * P * PACK], BF16, name="h_grouped", align_bytes=64, bufs=4)
+                h_grouped[u] = stage.tile([P, PAIR * P * PACK], BF16, name="h_grouped", align_bytes=64, bufs=12)
                 nc.scalar.copy(
                     out=h_grouped[u][:].bitcast(F32).rearrange("q (k b e) -> q k b e", k=PAIR, e=2),
                     in_=h_flipped[u][:].rearrange("q k e b -> q k b e"),
@@ -260,16 +261,18 @@ def tile_npertokenswishglu_basis_pb_t_kernel(tc, h, w_down_mix, out):
                 )
 
 
+            quantised = 0
             last = (PAIRS - 1) * 2 * PAIRS - WEIGHTS_FIRST + TURNED_AT["quantise"]
-            for step in range(-WEIGHTS_FIRST, max(UNITS + H_QUANTISE, last + 1)):
+            for step in range(-WEIGHTS_FIRST, max(UNITS + H_REGROUP, last + 1)):
                 if 0 <= step < UNITS:
                     flip_h(step)
                 weight_work("tensor", step)
                 if 0 <= step - H_REGROUP < UNITS:
                     regroup_h(step - H_REGROUP)
                 weight_work("scalar", step)
-                if 0 <= step - H_QUANTISE < UNITS:
-                    quantise_h(step - H_QUANTISE)
+                if quantised < (step - H_QUANTISE + 1) * H_SHARE and quantised < UNITS:
+                    quantise_h(quantised)
+                    quantised += 1
                 weight_work("vector", step)
 
         with tc.psum_pool(name="y_psum", bufs=2 * GROUP, reuse_waits="tile") as y_psum:
@@ -319,6 +322,9 @@ def tile_npertokenswishglu_basis_pb_t_kernel(tc, h, w_down_mix, out):
                     normed[g - 1] = results.tile([P, GROUP, FEATURES], F32, name="normed")
                     for k in range(GROUP - 1):
                         scale_rows(g - 1, k)
+                for u in range(quantised, min(quantised + 2, UNITS)):
+                    quantise_h(u)
+                quantised = min(quantised + 2, UNITS)
                 if g < GROUPS:
                     for k in range(1, GROUP):
                         row_sum(g, k)

@@ -29,12 +29,12 @@ WORDS = HIDDEN // 2
 FLOPS = 2 * BATCH * TOKENS * HIDDEN * FEATURES
 
 GROUP = 4
-GROUPS_PER_TILE = TOKENS // GROUP
-GROUPS = TILES * GROUPS_PER_TILE
+WHOLE_GROUPS = [(i, first, GROUP) for i in range(TILES) for first in range(0, TOKENS, GROUP)]
+GROUPS = WHOLE_GROUPS[:-1] + [(TILES - 1, TOKENS - 4, 2), (TILES - 1, TOKENS - 2, 2)]
 STORE_TOKENS = 2
 
-WEIGHTS_FIRST = 6
-DIAGONAL_AT = dict(gram=(0, 1, 2, 3), mask=4, ones=(6, 6, 7, 7), root=8, scale=(8, 9, 10, 11), quantise=13)
+WEIGHTS_FIRST = 12
+DIAGONAL_AT = dict(gram=(0, 2, 4, 6), mask=6, ones=(9, 11, 13, 15), root=15, scale=(16, 17, 18, 19), quantise=21)
 TURNED_AT = dict(flip=(1, 1, 5, 5), square=(2, 3, 6, 7), root=9, spread=(11, 11, 12, 12), scale=(12, 13, 14, 15), quantise=17)
 RUN = 4
 H_SHARE = 11 / 16
@@ -138,12 +138,10 @@ def tile_npertokenswishglu_basis_pb_t_kernel(tc, h, w_down_mix, out):
             def spread_turned(l, block):
                 if block == 0:
                     w_psum[l] = psum.tile([P, FEATURES], F32, name="w_spread", bufs=1)
-                nc.tensor.matmul(
+                nc.tensor.transpose(
                     out=w_psum[l][:, block * P : (block + 1) * P],
-                    lhsT=w_inverse[l][:, block : block + 1].to_broadcast([P, P]),
-                    rhs=ident_f32[:],
-                    start=True,
-                    stop=True,
+                    in_=w_inverse[l][:, block : block + 1].to_broadcast([P, P]),
+                    identity=ident_f32[:],
                 )
 
             def gram(l, block):
@@ -262,7 +260,7 @@ def tile_npertokenswishglu_basis_pb_t_kernel(tc, h, w_down_mix, out):
 
 
             quantised = 0
-            last = (PAIRS - 1) * 2 * PAIRS - WEIGHTS_FIRST + TURNED_AT["quantise"]
+            last = (PAIRS - 1) * 2 * PAIRS - WEIGHTS_FIRST + max(DIAGONAL_AT["quantise"], TURNED_AT["quantise"])
             for step in range(-WEIGHTS_FIRST, max(UNITS + H_REGROUP, last + 1)):
                 if 0 <= step < UNITS:
                     flip_h(step)
@@ -283,9 +281,9 @@ def tile_npertokenswishglu_basis_pb_t_kernel(tc, h, w_down_mix, out):
             normed = {}
 
             def multiply(g):
-                i = g // GROUPS_PER_TILE
-                for k in range(GROUP):
-                    l = (g % GROUPS_PER_TILE) * GROUP + k
+                i, first, count = GROUPS[g]
+                for k in range(count):
+                    l = first + k
                     y[g, k] = y_psum.tile([P, FEATURES], F32, name="y")
                     nc.tensor.matmul_mx(
                         out=y[g, k][:],
@@ -300,34 +298,44 @@ def tile_npertokenswishglu_basis_pb_t_kernel(tc, h, w_down_mix, out):
             def row_sum(g, k):
                 sum_of_squares(y[g, k][:], y_totals[g][:, k : k + 1])
 
-            def scale_rows(g, k):
-                nc.vector.tensor_scalar_mul(
-                    out=normed[g][:, k, :], in0=y[g, k][:], scalar1=y_inverse_norm[g][:, k : k + 1]
+            def store(g, k, count):
+                i, first = GROUPS[g][:2]
+                nc.sync.dma_start(
+                    out=out[i * P : (i + 1) * P, first + k : first + k + count, :], in_=normed[g][:, k : k + count, :]
                 )
-                if k % STORE_TOKENS == STORE_TOKENS - 1:
-                    i = g // GROUPS_PER_TILE
-                    last_token = (g % GROUPS_PER_TILE) * GROUP + k
-                    nc.sync.dma_start(
-                        out=out[i * P : (i + 1) * P, last_token + 1 - STORE_TOKENS : last_token + 1, :],
-                        in_=normed[g][:, k + 1 - STORE_TOKENS : k + 1, :],
-                    )
 
-            for g in range(GROUPS + 1):
-                if g < GROUPS:
+            def scale_rows(g, k):
+                out_rows = normed[g][:, k, :]
+                inverse = y_inverse_norm[g][:, k : k + 1]
+                if g < len(GROUPS) - 2 or k == 0:
+                    nc.vector.tensor_scalar_mul(out=out_rows, in0=y[g, k][:], scalar1=inverse)
+                else:
+                    nc.scalar.activation(out=out_rows, in_=y[g, k][:], func=ACT.Copy, scale=inverse)
+                if g == len(GROUPS) - 1:
+                    store(g, k, 1)
+                elif k % STORE_TOKENS == STORE_TOKENS - 1:
+                    store(g, k + 1 - STORE_TOKENS, STORE_TOKENS)
+
+            for g in range(len(GROUPS) + 1):
+                if g < len(GROUPS):
+                    count = GROUPS[g][2]
                     multiply(g)
-                    y_totals[g] = small.tile([P, GROUP], F32, name="y_totals")
+                    y_totals[g] = small.tile([P, count], F32, name="y_totals%d" % count)
                     row_sum(g, 0)
                 if g >= 1:
-                    y_inverse_norm[g - 1] = inverse_root(y_clamped[g - 1], GROUP)
+                    before = GROUPS[g - 1][2]
+                    y_inverse_norm[g - 1] = inverse_root(y_clamped[g - 1], before)
                     normed[g - 1] = results.tile([P, GROUP, FEATURES], F32, name="normed")
-                    for k in range(GROUP - 1):
+                    ahead = before if g == len(GROUPS) else min(before - 1, count)
+                    for k in range(ahead):
                         scale_rows(g - 1, k)
-                for u in range(quantised, min(quantised + 2, UNITS)):
-                    quantise_h(u)
-                quantised = min(quantised + 2, UNITS)
-                if g < GROUPS:
-                    for k in range(1, GROUP):
+                if quantised < UNITS:
+                    quantise_h(quantised)
+                    quantised += 1
+                if g < len(GROUPS):
+                    for k in range(1, count):
                         row_sum(g, k)
-                    y_clamped[g] = clamp(y_totals[g], GROUP)
+                    y_clamped[g] = clamp(y_totals[g], count)
                 if g >= 1:
-                    scale_rows(g - 1, GROUP - 1)
+                    for k in range(ahead, before):
+                        scale_rows(g - 1, k)

@@ -33,7 +33,10 @@ WHOLE_GROUPS = [(i, first, GROUP) for i in range(TILES) for first in range(0, TO
 GROUPS = WHOLE_GROUPS[:-1] + [(TILES - 1, TOKENS - 4, 2), (TILES - 1, TOKENS - 2, 2)]
 STORE_TOKENS = 2
 
-WEIGHTS_FIRST = 12
+WEIGHTS_FIRST = 8
+FIRST_DIAGONAL_AT = dict(gram=(0, 1, 2, 3), mask=4, ones=(5, 5, 5, 5), root=5, scale=(6, 7, 8, 9), quantise=13)
+FIRST_TURNED_AT = dict(flip=(1, 1, 3, 3), square=(2, 3, 4, 5), root=10, spread=(11, 11, 12, 12), scale=(12, 13, 14, 15), quantise=17)
+PAIR_STARTS = (0, 4, 12, 20)
 DIAGONAL_AT = dict(gram=(0, 2, 4, 6), mask=6, ones=(9, 11, 13, 15), root=15, scale=(16, 17, 18, 19), quantise=21)
 TURNED_AT = dict(flip=(1, 1, 5, 5), square=(2, 3, 6, 7), root=9, spread=(11, 11, 12, 12), scale=(12, 13, 14, 15), quantise=17)
 RUN = 4
@@ -71,13 +74,15 @@ def tile_npertokenswishglu_basis_pb_t_kernel(tc, h, w_down_mix, out):
 
         load_weight(0)
         load_weight(1)
+        load_weight(2)
+        load_weight(3)
         load_h(0, 0, 2)
         load_h(0, 2, 2)
         for i in range(1, TILES):
-            if PAIR * i < TOKENS:
-                load_weight(PAIR * i)
-                load_weight(PAIR * i + 1)
             load_h(i, 0, PAIRS)
+            if PAIR * (i + 1) < TOKENS:
+                load_weight(PAIR * (i + 1))
+                load_weight(PAIR * (i + 1) + 1)
 
         ident_bf16 = const.tile([P, P], BF16)
         make_identity(nc, ident_bf16[:])
@@ -117,7 +122,7 @@ def tile_npertokenswishglu_basis_pb_t_kernel(tc, h, w_down_mix, out):
 
             def flip_weight(l, block):
                 if block % 2 == 0:
-                    w_psum[l, block // 2] = psum.tile([P, 2, PACK, P], BF16, name="w_flipped", bufs=1)
+                    w_psum[l, block // 2] = psum.tile([P, 2, PACK, P], BF16, name="w_flipped", bufs=2)
                 for t in range(PACK):
                     nc.tensor.transpose(
                         out=w_psum[l, block // 2][:, block % 2, t, :],
@@ -137,7 +142,9 @@ def tile_npertokenswishglu_basis_pb_t_kernel(tc, h, w_down_mix, out):
 
             def spread_turned(l, block):
                 if block == 0:
-                    w_psum[l] = psum.tile([P, FEATURES], F32, name="w_spread", bufs=1)
+                    w_psum[l] = psum.tile(
+                        [P, FEATURES], F32, name="w_flipped" if l == 1 else "w_spread", bufs=2 if l == 1 else 1
+                    )
                 nc.tensor.transpose(
                     out=w_psum[l][:, block * P : (block + 1) * P],
                     in_=w_inverse[l][:, block : block + 1].to_broadcast([P, P]),
@@ -203,8 +210,11 @@ def tile_npertokenswishglu_basis_pb_t_kernel(tc, h, w_down_mix, out):
 
             def weight_work(engine, step):
                 for l in range(TOKENS):
-                    at = DIAGONAL_AT if l % 2 == 0 else TURNED_AT
-                    s = step + WEIGHTS_FIRST - (l // PAIR) * 2 * PAIRS
+                    if l < PAIR:
+                        at = FIRST_DIAGONAL_AT if l == 0 else FIRST_TURNED_AT
+                    else:
+                        at = DIAGONAL_AT if l % 2 == 0 else TURNED_AT
+                    s = step + WEIGHTS_FIRST - PAIR_STARTS[l // PAIR]
                     blocks = range(BLOCKS)
                     if engine == "tensor":
                         for name, work in (("gram", gram), ("ones", add_partitions), ("spread", spread_turned), ("flip", flip_weight)):
@@ -233,7 +243,7 @@ def tile_npertokenswishglu_basis_pb_t_kernel(tc, h, w_down_mix, out):
             h_grouped = {}
 
             def flip_h(u):
-                h_flipped[u] = psum.tile([P, PAIR, 2, P], F32, name="h_flipped", bufs=4)
+                h_flipped[u] = psum.tile([P, PAIR, 2, P], F32, name="h_flipped", bufs=3)
                 words = h_raw[u].bitcast(F32)
                 for k in range(PAIR):
                     for e in range(2):
@@ -259,8 +269,12 @@ def tile_npertokenswishglu_basis_pb_t_kernel(tc, h, w_down_mix, out):
                 )
 
 
+            idle = psum.tile([P, P], F32, name="h_flipped", bufs=3)
+            for repeat in range(5):
+                nc.tensor.matmul(out=idle[:], lhsT=ones[:], rhs=ones[:], start=True, stop=True)
+
             quantised = 0
-            last = (PAIRS - 1) * 2 * PAIRS - WEIGHTS_FIRST + max(DIAGONAL_AT["quantise"], TURNED_AT["quantise"])
+            last = PAIR_STARTS[-1] - WEIGHTS_FIRST + max(DIAGONAL_AT["quantise"], TURNED_AT["quantise"])
             for step in range(-WEIGHTS_FIRST, max(UNITS + H_REGROUP, last + 1)):
                 if 0 <= step < UNITS:
                     flip_h(step)

from contextlib import ExitStack

import concourse.mybir as mybir
from concourse.masks import make_identity

F32 = mybir.dt.float32
BF16 = mybir.dt.bfloat16
U32 = mybir.dt.uint32
U8 = mybir.dt.uint8
FP8X4 = mybir.dt.float8_e4m3fn_x4
ACT = mybir.ActivationFunctionType
ALU = mybir.AluOpType

P = 128
BATCH = 1024
TOKENS = 8
HIDDEN = 512
FEATURES = 512
PACK = 4
EPS = 1e-12

TILES = BATCH // P
BLOCKS = FEATURES // P
PAIR = 2
PAIRS = TOKENS // PAIR
UNITS = PAIRS * TILES
WORDS = HIDDEN // 2

FLOPS = 2 * BATCH * TOKENS * HIDDEN * FEATURES

GROUP = 4
WHOLE_GROUPS = [(i, first, GROUP) for i in range(TILES) for first in range(0, TOKENS, GROUP)]
GROUPS = WHOLE_GROUPS[:-1] + [(TILES - 1, TOKENS - 4, 2), (TILES - 1, TOKENS - 2, 2)]
STORE_TOKENS = 2

WEIGHTS_FIRST = 8
FIRST_DIAGONAL_AT = dict(gram=(0, 1, 2, 3), mask=4, ones=(5, 5, 5, 5), root=5, scale=(6, 7, 8, 9), quantise=13)
FIRST_TURNED_AT = dict(flip=(1, 1, 3, 3), square=(2, 3, 4, 5), root=10, spread=(11, 11, 12, 12), scale=(12, 13, 14, 15), quantise=17)
PAIR_STARTS = (0, 4, 12, 20)
DIAGONAL_AT = dict(gram=(0, 2, 4, 6), mask=6, ones=(9, 11, 13, 15), root=15, scale=(16, 17, 18, 19), quantise=21)
TURNED_AT = dict(flip=(1, 1, 5, 5), square=(2, 3, 6, 7), root=9, spread=(11, 11, 12, 12), scale=(12, 13, 14, 15), quantise=17)
RUN = 4
H_SHARE = 11 / 16
H_REGROUP, H_QUANTISE = 1, 2


def tile_npertokenswishglu_basis_pb_t_kernel(tc, h, w_down_mix, out):
    nc = tc.nc
    with ExitStack() as ctx:
        ctx.enter_context(tc.manual_schedule())
        const = ctx.enter_context(tc.tile_pool(name="const", bufs=1))
        raw = ctx.enter_context(tc.tile_pool(name="raw", bufs=1))
        weights = ctx.enter_context(tc.tile_pool(name="weights", bufs=1))
        stage = ctx.enter_context(tc.tile_pool(name="stage", bufs=2))
        small = ctx.enter_context(tc.tile_pool(name="small", bufs=4))
        results = ctx.enter_context(tc.tile_pool(name="results", bufs=4))

        w_raw = {}
        h_raw = {}

        def load_weight(l):
            w_raw[l] = raw.tile([P, PACK, FEATURES], BF16, name="w_raw%d" % l)
            nc.sync.dma_start(out=w_raw[l][:], in_=w_down_mix[l].rearrange("(q t) j -> q t j", t=PACK))

        def load_h(i, pair, count):
            width = PAIR * HIDDEN
            tile = raw.tile([P, count * width], BF16, name="h_raw%d_%d" % (i, pair))
            nc.sync.dma_start(
                out=tile[:].rearrange("b (l f) -> b l f", f=HIDDEN),
                in_=h[i * P : (i + 1) * P, PAIR * pair : PAIR * (pair + count), :],
            )
            for k in range(count):
                h_raw[i * PAIRS + pair + k] = tile[:, k * width : (k + 1) * width]

        load_weight(0)
        load_weight(1)
        load_weight(2)
        load_weight(3)
        load_h(0, 0, 2)
        load_h(0, 2, 2)
        for i in range(1, TILES):
            load_h(i, 0, PAIRS)
            if PAIR * (i + 1) < TOKENS:
                load_weight(PAIR * (i + 1))
                load_weight(PAIR * (i + 1) + 1)

        ident_bf16 = const.tile([P, P], BF16)
        make_identity(nc, ident_bf16[:])
        ident_f32 = const.tile([P, P], F32)
        make_identity(nc, ident_f32[:])
        ones = const.tile([P, P], F32)
        nc.vector.memset(ones[:], 1.0)

        warm = const.tile([P, 1], F32)
        nc.scalar.activation(out=warm[:], in_=ones[:, 0:1], func=ACT.Abs_reciprocal_sqrt)

        def sum_of_squares(values, total):
            squares = stage.tile([P, HIDDEN], BF16, name="squares", bufs=4)
            nc.scalar.activation(out=squares[:], in_=values, func=ACT.Square, accum_out=total)

        def clamp(totals, width):
            clamped = small.tile([P, width], F32, name="clamped%d" % width)
            nc.vector.tensor_scalar_max(out=clamped[:], in0=totals[:], scalar1=EPS * EPS)
            return clamped

        def inverse_root(clamped, width):
            inverse = small.tile([P, width], F32, name="inverse%d" % width)
            nc.scalar.activation(out=inverse[:], in_=clamped[:], func=ACT.Abs_reciprocal_sqrt)
            return inverse

        w_codes = [weights.tile([P, FEATURES], U32, name="w_codes%d" % l, align_bytes=64) for l in range(TOKENS)]
        w_scales = [weights.tile([P, FEATURES], U8, name="w_scales%d" % l, align_bytes=64) for l in range(TOKENS)]
        h_codes = [weights.tile([P, TOKENS * P], U32, name="h_codes%d" % i, align_bytes=64) for i in range(TILES)]
        h_scales = [weights.tile([P, TOKENS * P], U8, name="h_scales%d" % i, align_bytes=64) for i in range(TILES)]

        with tc.psum_pool(name="prep_psum", bufs=1) as psum:
            w_psum = {}
            w_totals = {}
            w_diagonal = {}
            w_inverse = {}
            nd = {}

            def flip_weight(l, block):
                if block % 2 == 0:
                    w_psum[l, block // 2] = psum.tile([P, 2, PACK, P], BF16, name="w_flipped", bufs=2)
                for t in range(PACK):
                    nc.tensor.transpose(
                        out=w_psum[l, block // 2][:, block % 2, t, :],
                        in_=w_raw[l][:, t, block * P : (block + 1) * P],
                        identity=ident_bf16[:],
                    )

            def square_weight(l, block):
                if block == 0:
                    w_totals[l] = small.tile([P, BLOCKS], F32, name="w_totals")
                sum_of_squares(
                    w_psum[l, block // 2][:, block % 2].rearrange("j t q -> j (t q)"), w_totals[l][:, block : block + 1]
                )

            def root_turned(l):
                w_inverse[l] = inverse_root(clamp(w_totals[l], BLOCKS), BLOCKS)

            def spread_turned(l, block):
                if block == 0:
                    w_psum[l] = psum.tile(
                        [P, FEATURES], F32, name="w_flipped" if l == 1 else "w_spread", bufs=2 if l == 1 else 1
                    )
                nc.tensor.transpose(
                    out=w_psum[l][:, block * P : (block + 1) * P],
                    in_=w_inverse[l][:, block : block + 1].to_broadcast([P, P]),
                    identity=ident_f32[:],
                )

            def gram(l, block):
                if block == 0:
                    w_psum[l] = psum.tile([P, BLOCKS, P], F32, name="w_sums", bufs=2)
                for t in range(PACK):
                    columns = w_raw[l][:, t, block * P : (block + 1) * P]
                    nc.tensor.matmul(
                        out=w_psum[l][:, block, :], lhsT=columns, rhs=columns, start=t == 0, stop=t == PACK - 1
                    )

            def mask(l):
                w_diagonal[l] = stage.tile([P, BLOCKS, P], F32, name="w_diagonal")
                nc.vector.scalar_tensor_tensor(
                    out=w_diagonal[l][:],
                    in0=w_psum[l][:],
                    scalar=EPS * EPS,
                    in1=ident_f32[:].unsqueeze(1).to_broadcast([P, BLOCKS, P]),
                    op0=ALU.max,
                    op1=ALU.mult,
                )

            def add_partitions(l, block):
                if block == 0:
                    w_psum[l] = psum.tile([P, FEATURES], F32, name="w_sums", bufs=2)
                nc.tensor.matmul(
                    out=w_psum[l][:, block * P : (block + 1) * P],
                    lhsT=ones[:],
                    rhs=w_diagonal[l][:, block, :],
                    start=True,
                    stop=True,
                )

            def root_gram(l):
                w_inverse[l] = stage.tile([P, FEATURES], F32, name="w_inverse")
                nc.scalar.activation(out=w_inverse[l][:], in_=w_psum[l][:], func=ACT.Abs_reciprocal_sqrt)

            def scale_weight(l, block):
                if block == 0:
                    nd[l] = stage.tile([P, FEATURES, PACK], BF16, name="nd", align_bytes=64)
                columns = slice(block * P, (block + 1) * P)
                inverse = w_inverse[l] if l % 2 == 0 else w_psum[l]
                nc.vector.tensor_tensor(
                    out=nd[l][:, columns, :].rearrange("q (c i) t -> q c t i", i=RUN),
                    in0=w_raw[l][:, :, columns].rearrange("q t (c i) -> q c t i", i=RUN),
                    in1=inverse[:, columns]
                    .rearrange("q (c i) -> q c i", i=RUN)
                    .unsqueeze(2)
                    .to_broadcast([P, P // RUN, PACK, RUN]),
                    op=ALU.mult,
                )

            def quantise_weight(l):
                nc.vector.quantize_mx(
                    out=w_codes[l][:].bitcast(FP8X4),
                    scales=w_scales[l][:],
                    in_=nd[l][:].rearrange("q j t -> q (j t)"),
                )

            def weight_work(engine, step):
                for l in range(TOKENS):
                    if l < PAIR:
                        at = FIRST_DIAGONAL_AT if l == 0 else FIRST_TURNED_AT
                    else:
                        at = DIAGONAL_AT if l % 2 == 0 else TURNED_AT
                    s = step + WEIGHTS_FIRST - PAIR_STARTS[l // PAIR]
                    blocks = range(BLOCKS)
                    if engine == "tensor":
                        for name, work in (("gram", gram), ("ones", add_partitions), ("spread", spread_turned), ("flip", flip_weight)):
                            for block in blocks:
                                if name in at and at[name][block] == s:
                                    work(l, block)
                    elif engine == "scalar":
                        for block in blocks:
                            if "square" in at and at["square"][block] == s:
                                square_weight(l, block)
                        if at["root"] == s:
                            if l % 2 == 0:
                                root_gram(l)
                            else:
                                root_turned(l)
                    else:
                        if at.get("mask") == s:
                            mask(l)
                        for block in blocks:
                            if at["scale"][block] == s:
                                scale_weight(l, block)
                        if at["quantise"] == s:
                            quantise_weight(l)

            h_flipped = {}
            h_grouped = {}

            def flip_h(u):
                h_flipped[u] = psum.tile([P, PAIR, 2, P], F32, name="h_flipped", bufs=3)
                words = h_raw[u].bitcast(F32)
                for k in range(PAIR):
                    for e in range(2):
                        nc.tensor.transpose(
                            out=h_flipped[u][:, k, e, :],
                            in_=words[:, k * WORDS + e : (k + 1) * WORDS : 2],
                            identity=ident_f32[:],
                        )

            def regroup_h(u):
                h_grouped[u] = stage.tile([P, PAIR * P * PACK], BF16, name="h_grouped", align_bytes=64, bufs=12)
                nc.scalar.copy(
                    out=h_grouped[u][:].bitcast(F32).rearrange("q (k b e) -> q k b e", k=PAIR, e=2),
                    in_=h_flipped[u][:].rearrange("q k e b -> q k b e"),
                )

            def quantise_h(u):
                columns = slice((u % PAIRS) * PAIR * P, (u % PAIRS + 1) * PAIR * P)
                nc.vector.quantize_mx(
                    out=h_codes[u // PAIRS][:, columns].bitcast(FP8X4),
                    scales=h_scales[u // PAIRS][:, columns],
                    in_=h_grouped[u][:],
                )


            idle = psum.tile([P, P], F32, name="h_flipped", bufs=3)
            for repeat in range(5):
                nc.tensor.matmul(out=idle[:], lhsT=ones[:], rhs=ones[:], start=True, stop=True)

            quantised = 0
            last = PAIR_STARTS[-1] - WEIGHTS_FIRST + max(DIAGONAL_AT["quantise"], TURNED_AT["quantise"])
            for step in range(-WEIGHTS_FIRST, max(UNITS + H_REGROUP, last + 1)):
                if 0 <= step < UNITS:
                    flip_h(step)
                weight_work("tensor", step)
                if 0 <= step - H_REGROUP < UNITS:
                    regroup_h(step - H_REGROUP)
                weight_work("scalar", step)
                if quantised < (step - H_QUANTISE + 1) * H_SHARE and quantised < UNITS:
                    quantise_h(quantised)
                    quantised += 1
                weight_work("vector", step)

        with tc.psum_pool(name="y_psum", bufs=2 * GROUP, reuse_waits="tile") as y_psum:
            y = {}
            y_totals = {}
            y_clamped = {}
            y_inverse_norm = {}
            normed = {}

            def multiply(g):
                i, first, count = GROUPS[g]
                for k in range(count):
                    l = first + k
                    y[g, k] = y_psum.tile([P, FEATURES], F32, name="y")
                    nc.tensor.matmul_mx(
                        out=y[g, k][:],
                        lhsT=h_codes[i][:, l * P : (l + 1) * P].bitcast(FP8X4),
                        lhsT_scale=h_scales[i][:, l * P : (l + 1) * P],
                        rhs=w_codes[l][:].bitcast(FP8X4),
                        rhs_scale=w_scales[l][:],
                        start=True,
                        stop=True,
                    )

            def row_sum(g, k):
                sum_of_squares(y[g, k][:], y_totals[g][:, k : k + 1])

            def store(g, k, count):
                i, first = GROUPS[g][:2]
                nc.sync.dma_start(
                    out=out[i * P : (i + 1) * P, first + k : first + k + count, :], in_=normed[g][:, k : k + count, :]
                )

            def scale_rows(g, k):
                out_rows = normed[g][:, k, :]
                inverse = y_inverse_norm[g][:, k : k + 1]
                if g < len(GROUPS) - 2 or k == 0:
                    nc.vector.tensor_scalar_mul(out=out_rows, in0=y[g, k][:], scalar1=inverse)
                else:
                    nc.scalar.activation(out=out_rows, in_=y[g, k][:], func=ACT.Copy, scale=inverse)
                if g == len(GROUPS) - 1:
                    store(g, k, 1)
                elif k % STORE_TOKENS == STORE_TOKENS - 1:
                    store(g, k + 1 - STORE_TOKENS, STORE_TOKENS)

            for g in range(len(GROUPS) + 1):
                if g < len(GROUPS):
                    count = GROUPS[g][2]
                    multiply(g)
                    y_totals[g] = small.tile([P, count], F32, name="y_totals%d" % count)
                    row_sum(g, 0)
                if g >= 1:
                    before = GROUPS[g - 1][2]
                    y_inverse_norm[g - 1] = inverse_root(y_clamped[g - 1], before)
                    normed[g - 1] = results.tile([P, GROUP, FEATURES], F32, name="normed")
                    ahead = before if g == len(GROUPS) else min(before - 1, count)
                    for k in range(ahead):
                        scale_rows(g - 1, k)
                if quantised < UNITS:
                    quantise_h(quantised)
                    quantised += 1
                if g < len(GROUPS):
                    for k in range(1, count):
                        row_sum(g, k)
                    y_clamped[g] = clamp(y_totals[g], count)
                if g >= 1:
                    for k in range(ahead, before):
                        scale_rows(g - 1, k)
